import numpy as np
import ml_dtypes


def mxq(x, axis, fmt="e4m3"):
    dtype, down = {"e4m3": (ml_dtypes.float8_e4m3fn, 7), "e5m2": (ml_dtypes.float8_e5m2, 14)}[fmt]
    v = np.moveaxis(np.asarray(x, np.float32).astype(ml_dtypes.bfloat16).astype(np.float64), axis, -1)
    blocks = v.reshape(v.shape[:-1] + (-1, 32))
    amax = np.abs(blocks).max(-1, keepdims=True)
    byte = np.maximum(np.where(amax > 0, np.frexp(amax)[1] - 1 + 127, 0) - down, 1)
    scale = np.exp2(byte - 127.0)
    codes = (blocks / scale).astype(np.float32).astype(dtype).astype(np.float64)
    return np.moveaxis((codes * scale).reshape(v.shape), -1, axis)


WIDE = False


def mx_kscale(k):
    if not WIDE:
        return np.ones(k)
    levels = np.array([10, -10, 5, -5, 0])
    if k % 512:
        return np.exp2(np.random.permutation(np.resize(levels, k // 32))).repeat(32)
    a = np.empty((k // 512, 16))
    for p in range(k // 512):
        a[p, :8] = np.random.permutation(np.resize(levels, 8))
        for g in range(8):
            far = levels[np.abs(levels - a[p, g]) >= 10]
            a[p, g + 8] = far[np.random.randint(len(far))]
    return np.exp2(a.ravel()).repeat(32)


BF16 = ml_dtypes.bfloat16


def bf(x):
    return np.asarray(x, np.float32).astype(BF16)


def f64(x):
    return np.asarray(x).astype(np.float64)


B, T, N, DH, D = 4, 1024, 16, 32, 512
KC = N * DH


def setup_inputs():
    r = np.random.standard_normal
    s = mx_kscale(D)
    t = mx_kscale(KC).reshape(N, DH)
    return {"normalized_resid_pre": bf(r((B, T, D)) * s),
            "W_C": bf(r((N, D, DH)) / np.sqrt(D) / s[None, :, None] * t[:, None, :]),
            "b_C": bf(0.1 * r((N, DH)) * t),
            "W_K": bf(1.3 / np.sqrt(KC) * r((N, DH, DH, DH)) / t[:, None, None, :])}


def reference(normalized_resid_pre, W_C, b_C, W_K):
    x = f64(normalized_resid_pre)
    wc = f64(W_C).transpose(1, 0, 2).reshape(D, KC)
    c = (mxq(x, 2, "e4m3") @ mxq(wc, 0, "e4m3")) + f64(b_C).reshape(KC)
    wk = f64(W_K).transpose(0, 3, 1, 2).reshape(KC, DH * DH)
    step1 = mxq(c, 2, "e4m3") @ mxq(wk, 0, "e4m3")
    return step1.reshape(B, T, DH, DH)

@@ -1,0 +1,266 @@
+from contextlib import ExitStack
+
+import concourse.mybir as mybir
+from concourse.masks import make_identity
+
+FP8X4 = mybir.dt.float8_e4m3fn_x4
+BF16 = mybir.dt.bfloat16
+F32 = mybir.dt.float32
+U32 = mybir.dt.uint32
+U8 = mybir.dt.uint8
+ADD = mybir.AluOpType.add
+
+P = 128
+ROWS = 4096
+D = 512
+KC = 512
+IJ = 1024
+NT = ROWS // P
+FLOPS = 2 * ROWS * D * KC + 2 * ROWS * KC * IJ
+
+X_LOADS = [2, 2, 4, 8, 16]
+X_CHUNKS = [2, 2, 4, 4, 4, 4, 4, 4, 4]
+N_PRE = 3
+O_CHUNKS = [1] * 32
+D1 = 3
+DT = 6
+
+
+def a_on_scalar(xc):
+    return 1 <= xc <= 3
+
+
+def e_on_vector(g, half):
+    return half == 1 and g >= NT - D1
+
+
+def starts(sizes):
+    return [sum(sizes[:i]) for i in range(len(sizes))]
+
+
+def tile_trittentioncube_pb_t_kernel(tc, normalized_resid_pre, W_C, b_C, W_K, out):
+    nc = tc.nc
+    x_v = normalized_resid_pre.rearrange("b t d -> (b t) d").rearrange("(p t) d -> p t d", t=NT)
+    out_v = out.rearrange("b t i j -> (b t) (i j)").rearrange("(p t) f -> p t f", t=NT)
+    wc_v = W_C.rearrange("n (p t) k -> p n (t k)", t=4)
+    wk_v = W_K.rearrange("n i j k -> n (i j) k").rearrange("n (q s) k -> q n (s k)", s=8)
+    b_v = b_C.rearrange("n k -> (n k)").rearrange("(p t) -> p t", t=4)
+    x_first = starts(X_CHUNKS)
+    o_first = starts(O_CHUNKS)
+    x_of = [xc for xc, n in enumerate(X_CHUNKS) for a in range(n)]
+    o_of = [oc for oc, n in enumerate(O_CHUNKS) for a in range(n)]
+
+    with ExitStack() as ctx:
+        keep = ctx.enter_context(tc.tile_pool(name="keep", bufs=1))
+        work = ctx.enter_context(tc.tile_pool(name="work", bufs=3))
+        xcodes = ctx.enter_context(tc.tile_pool(name="xcodes", bufs=4))
+        ccodes = ctx.enter_context(tc.tile_pool(name="ccodes", bufs=6))
+        outs = ctx.enter_context(tc.tile_pool(name="outs", bufs=12))
+        psum = ctx.enter_context(tc.psum_pool(name="psum", bufs=2))
+        ctx.enter_context(tc.manual_schedule())
+
+        x_tiles = []
+        x_where = []
+        for i, n_tt in enumerate(X_LOADS):
+            x_tiles.append(keep.tile([P, n_tt, D], BF16, name="x%d" % i))
+            for a in range(n_tt):
+                x_where.append((i, a))
+        wc_raw = keep.tile([P, 2048], BF16, name="wc_raw")
+        b_raw = keep.tile([P, 4], BF16, name="b_raw")
+        wk_raw = [keep.tile([P, 8, 256], BF16, name="wk_raw%d" % h) for h in range(2)]
+
+        for h in range(2):
+            nc.sync.dma_start(out=wk_raw[h][:], in_=wk_v[:, 8 * h : 8 * h + 8, :])
+        nc.sync.dma_start(out=x_tiles[0][:], in_=x_v[:, 0 : X_LOADS[0], :])
+        nc.sync.dma_start(out=wc_raw[:].rearrange("p (a b) -> p a b", b=128), in_=wc_v)
+        nc.sync.dma_start(out=b_raw[:], in_=b_v)
+        t0 = X_LOADS[0]
+        for i in range(1, len(X_LOADS)):
+            nc.sync.dma_start(out=x_tiles[i][:], in_=x_v[:, t0 : t0 + X_LOADS[i], :])
+            t0 += X_LOADS[i]
+
+        ident = keep.tile([P, P], F32, name="ident")
+        make_identity(nc, ident[:])
+
+        xg = {}
+        xq = {}
+        cg = {}
+        cq = {}
+        pts = {}
+        pcs = {}
+        pos = {}
+        obs = {}
+
+        def t_pe(xc):
+            xg[xc] = work.tile([P, 2048], BF16, name="xg", tag="xg", align_bytes=64)
+            n = X_CHUNKS[xc]
+            for h in range((n + 1) // 2):
+                w = min(2, n - 2 * h)
+                pt = psum.tile([P, 2, 2 * P], F32, name="pt", tag="pt")
+                pts[(xc, h)] = (pt, w)
+                for a in range(w):
+                    i, loc = x_where[x_first[xc] + 2 * h + a]
+                    xw = x_tiles[i][:].bitcast(F32)
+                    for u in range(2):
+                        nc.tensor.transpose(
+                            pt[:, u, a * P : (a + 1) * P], xw[:, loc, u : 2 * P : 2], ident[:]
+                        )
+
+        def a_copy(xc, h):
+            pt, w = pts[(xc, h)]
+            xg_w = xg[xc][:].bitcast(F32).rearrange("p (w u) -> p w u", u=2)
+            dst = xg_w[:, h * 2 * P : h * 2 * P + w * P, :]
+            src = pt[:, :, 0 : w * P].rearrange("p u w -> p w u")
+            if a_on_scalar(xc):
+                nc.scalar.copy(out=dst, in_=src)
+            else:
+                nc.vector.tensor_copy(out=dst, in_=src)
+
+        def qx(xc):
+            n = X_CHUNKS[xc]
+            q = xcodes.tile([P, 512], U32, name="xq", tag="xq", align_bytes=64)
+            s = xcodes.tile([P, 512], U8, name="xs", tag="xs", align_bytes=64)
+            nc.vector.quantize_mx(
+                out=q[:, 0 : n * P].bitcast(FP8X4), scales=s[:, 0 : n * P], in_=xg[xc][:, 0 : 4 * n * P]
+            )
+            xq[xc] = (q, s)
+
+        def s1_pe(g):
+            q, s = xq[x_of[g]]
+            a = g - x_first[x_of[g]]
+            blk = slice(a * P, (a + 1) * P)
+            pc = psum.tile([P, 4, P], F32, name="pc", tag="pc")
+            pcs[g] = pc
+            for j in range(4):
+                cols = slice(j * P, (j + 1) * P)
+                nc.tensor.matmul_mx(
+                    out=pc[:, j, :],
+                    lhsT=wcq[:, cols].bitcast(FP8X4),
+                    lhsT_scale=wcs[:, cols],
+                    rhs=q[:, blk].bitcast(FP8X4),
+                    rhs_scale=s[:, blk],
+                    start=True,
+                    stop=True,
+                )
+
+        def c_copy(g):
+            cg[g] = work.tile([P, P, 4], BF16, name="cg", tag="cg", align_bytes=64)
+            nc.vector.tensor_tensor(
+                out=cg[g][:],
+                in0=pcs[g][:].rearrange("p j r -> p r j"),
+                in1=bias[:].unsqueeze(1).to_broadcast([P, P, 4]),
+                op=ADD,
+            )
+
+        def qc(g):
+            q = ccodes.tile([P, P], U32, name="cq", tag="cq", align_bytes=64)
+            s = ccodes.tile([P, P], U8, name="cs", tag="cs", align_bytes=64)
+            nc.vector.quantize_mx(
+                out=q[:].bitcast(FP8X4), scales=s[:], in_=cg[g][:].rearrange("p r j -> p (r j)")
+            )
+            cq[g] = (q, s)
+
+        def s2_pe(g):
+            q, s = cq[g]
+            for half in range(2):
+                cols = slice(half * 512, (half + 1) * 512)
+                po = psum.tile([P, 512], F32, name="po", tag="po", bufs=4)
+                pos[(g, half)] = po
+                nc.tensor.matmul_mx(
+                    out=po[:],
+                    lhsT=q[:].bitcast(FP8X4),
+                    lhsT_scale=s[:],
+                    rhs=wkq[:, cols].bitcast(FP8X4),
+                    rhs_scale=wks[:, cols],
+                    start=True,
+                    stop=True,
+                )
+
+        def e_copy(g):
+            oc = o_of[g]
+            a = g - o_first[oc]
+            if a == 0:
+                obs[oc] = outs.tile([P, 1, IJ], F32, name="ob", tag="ob")
+            for half in range(2):
+                cols = slice(half * 512, (half + 1) * 512)
+                if e_on_vector(g, half):
+                    nc.vector.tensor_copy(out=obs[oc][:, a, cols], in_=pos[(g, half)][:])
+                else:
+                    nc.scalar.copy(out=obs[oc][:, a, cols], in_=pos[(g, half)][:])
+            n = O_CHUNKS[oc]
+            if a == n - 1:
+                nc.sync.dma_start(out=out_v[:, o_first[oc] : o_first[oc] + n, :], in_=obs[oc][:, 0:n, :])
+
+        wk_s1 = keep.tile([P, 8, 256], F32, name="wk_s1")
+        wkg = keep.tile([P, 4 * IJ], BF16, name="wkg", align_bytes=64)
+        wkq = keep.tile([P, IJ], U32, name="wkq", align_bytes=64)
+        wks = keep.tile([P, IJ], U8, name="wks", align_bytes=64)
+        for h in range(2):
+            for u in range(2):
+                nc.scalar.copy(
+                    out=wk_s1[:, :, u * P + h * 64 : u * P + h * 64 + 64].rearrange("p s (n k) -> p s n k", n=8),
+                    in_=wk_raw[h][:].bitcast(F32).rearrange("p n (s k u) -> p u s n k", s=8, u=2)[:, u],
+                )
+        t_pe(0)
+        wkg_w = wkg[:].bitcast(F32).rearrange("p (q s u) -> p q s u", s=8, u=2)
+        pws = []
+        for b in range(4):
+            pw = psum.tile([P, 4, P], F32, name="pw", tag="po", bufs=4)
+            pws.append(pw)
+            for s2 in range(2):
+                for u in range(2):
+                    nc.tensor.transpose(
+                        pw[:, 2 * s2 + u, :], wk_s1[:, 2 * b + s2, u * P : (u + 1) * P], ident[:]
+                    )
+        for xc in range(1, N_PRE):
+            t_pe(xc)
+        a_copy(0, 0)
+        qx(0)
+        for b in range(4):
+            nc.scalar.copy(
+                out=wkg_w[:, :, 2 * b : 2 * b + 2, :], in_=pws[b][:].rearrange("p (s u) q -> p q s u", u=2)
+            )
+        for xc in range(1, N_PRE):
+            for h in range((X_CHUNKS[xc] + 1) // 2):
+                a_copy(xc, h)
+
+        bias = keep.tile([P, 4], F32, name="bias")
+        wcg = keep.tile([P, 2048], BF16, name="wcg", align_bytes=64)
+        wcq = keep.tile([P, 512], U32, name="wcq", align_bytes=64)
+        wcs = keep.tile([P, 512], U8, name="wcs", align_bytes=64)
+        raw_v = wc_raw[:].rearrange("p (n t k j) -> p j n k t", n=16, t=4, j=4)
+        wcg_v = wcg[:].rearrange("p (j n k t) -> p j n k t", j=4, n=16, t=4)
+        for j in range(4):
+            nc.vector.tensor_copy(out=wcg_v[:, j], in_=raw_v[:, j])
+        nc.vector.quantize_mx(out=wcq[:].bitcast(FP8X4), scales=wcs[:], in_=wcg[:])
+        nc.vector.tensor_copy(out=bias[:], in_=b_raw[:])
+
+        t_tick = [-1 if xc < N_PRE else max(0, x_first[xc] - DT) for xc in range(len(X_CHUNKS))]
+        for g1 in range(NT + D1):
+            g = g1 - D1
+            if g >= 0:
+                s2_pe(g)
+            if g1 < NT:
+                s1_pe(g1)
+            for xc in range(N_PRE, len(X_CHUNKS)):
+                if t_tick[xc] == g1:
+                    t_pe(xc)
+            if g1 < NT:
+                c_copy(g1)
+            if g1 == 0:
+                qx(1)
+            if g1 == 1:
+                nc.vector.quantize_mx(out=wkq[:].bitcast(FP8X4), scales=wks[:], in_=wkg[:])
+            if g1 == 2:
+                qx(2)
+            for xc in range(N_PRE, len(X_CHUNKS)):
+                if t_tick[xc] == g1:
+                    a_copy(xc, 0)
+                if t_tick[xc] + 1 == g1:
+                    a_copy(xc, 1)
+                if t_tick[xc] + 2 == g1:
+                    qx(xc)
+            if g1 < NT:
+                qc(g1)
+            if g >= 0:
+                e_copy(g)

@@ -23,7 +23,7 @@ X_CHUNKS = [2, 2, 4, 4, 4, 4, 4, 4, 4]
 N_PRE = 3
 O_CHUNKS = [1] * 32
 D1 = 3
-DT = 6
+DT = 7
 
 
 def a_on_scalar(xc):
@@ -234,6 +234,7 @@ def tile_trittentioncube_pb_t_kernel(tc, normalized_resid_pre, W_C, b_C, W_K, ou
             nc.vector.tensor_copy(out=wcg_v[:, j], in_=raw_v[:, j])
         nc.vector.quantize_mx(out=wcq[:].bitcast(FP8X4), scales=wcs[:], in_=wcg[:])
         nc.vector.tensor_copy(out=bias[:], in_=b_raw[:])
+        nc.vector.quantize_mx(out=wkq[:].bitcast(FP8X4), scales=wks[:], in_=wkg[:])
 
         t_tick = [-1 if xc < N_PRE else max(0, x_first[xc] - DT) for xc in range(len(X_CHUNKS))]
         for g1 in range(NT + D1):
@@ -249,8 +250,6 @@ def tile_trittentioncube_pb_t_kernel(tc, normalized_resid_pre, W_C, b_C, W_K, ou
                 c_copy(g1)
             if g1 == 0:
                 qx(1)
-            if g1 == 1:
-                nc.vector.quantize_mx(out=wkq[:].bitcast(FP8X4), scales=wks[:], in_=wkg[:])
             if g1 == 2:
                 qx(2)
             for xc in range(N_PRE, len(X_CHUNKS)):

@@ -21,7 +21,7 @@ FLOPS = 2 * ROWS * D * KC + 2 * ROWS * KC * IJ
 X_LOADS = [2, 2, 4, 8, 16]
 X_CHUNKS = [2, 2, 4, 4, 4, 4, 4, 4, 4]
 N_PRE = 3
-O_CHUNKS = [1] * 32
+O_CHUNKS = [1] * 12 + [2] * 9 + [1] * 2
 D1 = 3
 DT = 7
 
@@ -55,7 +55,7 @@ def tile_trittentioncube_pb_t_kernel(tc, normalized_resid_pre, W_C, b_C, W_K, ou
         work = ctx.enter_context(tc.tile_pool(name="work", bufs=3))
         xcodes = ctx.enter_context(tc.tile_pool(name="xcodes", bufs=4))
         ccodes = ctx.enter_context(tc.tile_pool(name="ccodes", bufs=6))
-        outs = ctx.enter_context(tc.tile_pool(name="outs", bufs=12))
+        outs = ctx.enter_context(tc.tile_pool(name="outs", bufs=10))
         psum = ctx.enter_context(tc.psum_pool(name="psum", bufs=2))
         ctx.enter_context(tc.manual_schedule())
 
@@ -180,7 +180,7 @@ def tile_trittentioncube_pb_t_kernel(tc, normalized_resid_pre, W_C, b_C, W_K, ou
             oc = o_of[g]
             a = g - o_first[oc]
             if a == 0:
-                obs[oc] = outs.tile([P, 1, IJ], F32, name="ob", tag="ob")
+                obs[oc] = outs.tile([P, 2, IJ], F32, name="ob", tag="ob")
             for half in range(2):
                 cols = slice(half * 512, (half + 1) * 512)
                 if e_on_vector(g, half):

@@ -21,7 +21,7 @@ FLOPS = 2 * ROWS * D * KC + 2 * ROWS * KC * IJ
 X_LOADS = [2, 2, 4, 8, 16]
 X_CHUNKS = [2, 2, 4, 4, 4, 4, 4, 4, 4]
 N_PRE = 3
-O_CHUNKS = [1] * 12 + [2] * 9 + [1] * 2
+O_CHUNKS = [1] * 4 + [2] * 14
 D1 = 3
 DT = 7
 
@@ -116,14 +116,16 @@ def tile_trittentioncube_pb_t_kernel(tc, normalized_resid_pre, W_C, b_C, W_K, ou
             else:
                 nc.vector.tensor_copy(out=dst, in_=src)
 
-        def qx(xc):
-            n = X_CHUNKS[xc]
-            q = xcodes.tile([P, 512], U32, name="xq", tag="xq", align_bytes=64)
-            s = xcodes.tile([P, 512], U8, name="xs", tag="xs", align_bytes=64)
+        def qx(xc, h=0):
+            if h == 0:
+                q = xcodes.tile([P, 512], U32, name="xq", tag="xq", align_bytes=256)
+                s = xcodes.tile([P, 512], U8, name="xs", tag="xs", align_bytes=256)
+                xq[xc] = (q, s)
+            q, s = xq[xc]
+            cols = slice(h * 256, (h + 1) * 256)
             nc.vector.quantize_mx(
-                out=q[:, 0 : n * P].bitcast(FP8X4), scales=s[:, 0 : n * P], in_=xg[xc][:, 0 : 4 * n * P]
+                out=q[:, cols].bitcast(FP8X4), scales=s[:, cols], in_=xg[xc][:, h * 1024 : (h + 1) * 1024]
             )
-            xq[xc] = (q, s)
 
         def s1_pe(g):
             q, s = xq[x_of[g]]
@@ -153,8 +155,8 @@ def tile_trittentioncube_pb_t_kernel(tc, normalized_resid_pre, W_C, b_C, W_K, ou
             )
 
         def qc(g):
-            q = ccodes.tile([P, P], U32, name="cq", tag="cq", align_bytes=64)
-            s = ccodes.tile([P, P], U8, name="cs", tag="cs", align_bytes=64)
+            q = ccodes.tile([P, P], U32, name="cq", tag="cq", align_bytes=256)
+            s = ccodes.tile([P, P], U8, name="cs", tag="cs", align_bytes=256)
             nc.vector.quantize_mx(
                 out=q[:].bitcast(FP8X4), scales=s[:], in_=cg[g][:].rearrange("p r j -> p (r j)")
             )
@@ -193,8 +195,8 @@ def tile_trittentioncube_pb_t_kernel(tc, normalized_resid_pre, W_C, b_C, W_K, ou
 
         wk_s1 = keep.tile([P, 8, 256], F32, name="wk_s1")
         wkg = keep.tile([P, 4 * IJ], BF16, name="wkg", align_bytes=64)
-        wkq = keep.tile([P, IJ], U32, name="wkq", align_bytes=64)
-        wks = keep.tile([P, IJ], U8, name="wks", align_bytes=64)
+        wkq = keep.tile([P, IJ], U32, name="wkq", align_bytes=256)
+        wks = keep.tile([P, IJ], U8, name="wks", align_bytes=256)
         for h in range(2):
             for u in range(2):
                 nc.scalar.copy(
@@ -226,8 +228,8 @@ def tile_trittentioncube_pb_t_kernel(tc, normalized_resid_pre, W_C, b_C, W_K, ou
 
         bias = keep.tile([P, 4], F32, name="bias")
         wcg = keep.tile([P, 2048], BF16, name="wcg", align_bytes=64)
-        wcq = keep.tile([P, 512], U32, name="wcq", align_bytes=64)
-        wcs = keep.tile([P, 512], U8, name="wcs", align_bytes=64)
+        wcq = keep.tile([P, 512], U32, name="wcq", align_bytes=256)
+        wcs = keep.tile([P, 512], U8, name="wcs", align_bytes=256)
         raw_v = wc_raw[:].rearrange("p (n t k j) -> p j n k t", n=16, t=4, j=4)
         wcg_v = wcg[:].rearrange("p (j n k t) -> p j n k t", j=4, n=16, t=4)
         for j in range(4):
@@ -236,7 +238,7 @@ def tile_trittentioncube_pb_t_kernel(tc, normalized_resid_pre, W_C, b_C, W_K, ou
         nc.vector.tensor_copy(out=bias[:], in_=b_raw[:])
         nc.vector.quantize_mx(out=wkq[:].bitcast(FP8X4), scales=wks[:], in_=wkg[:])
 
-        t_tick = [-1 if xc < N_PRE else max(0, x_first[xc] - DT) for xc in range(len(X_CHUNKS))]
+        t_tick = [-1 if xc < N_PRE else 1 + 14 * (xc - N_PRE) // 3 for xc in range(len(X_CHUNKS))]
         for g1 in range(NT + D1):
             g = g1 - D1
             if g >= 0:
@@ -252,13 +254,15 @@ def tile_trittentioncube_pb_t_kernel(tc, normalized_resid_pre, W_C, b_C, W_K, ou
                 qx(1)
             if g1 == 2:
                 qx(2)
+                qx(2, 1)
             for xc in range(N_PRE, len(X_CHUNKS)):
                 if t_tick[xc] == g1:
                     a_copy(xc, 0)
                 if t_tick[xc] + 1 == g1:
                     a_copy(xc, 1)
-                if t_tick[xc] + 2 == g1:
-                    qx(xc)
+                for h in range(2):
+                    if t_tick[xc] + 2 + h == g1:
+                        qx(xc, h)
             if g1 < NT:
                 qc(g1)
             if g >= 0:

from contextlib import ExitStack

import concourse.mybir as mybir
from concourse.masks import make_identity

FP8X4 = mybir.dt.float8_e4m3fn_x4
BF16 = mybir.dt.bfloat16
F32 = mybir.dt.float32
U32 = mybir.dt.uint32
U8 = mybir.dt.uint8
ADD = mybir.AluOpType.add

P = 128
ROWS = 4096
D = 512
KC = 512
IJ = 1024
NT = ROWS // P
FLOPS = 2 * ROWS * D * KC + 2 * ROWS * KC * IJ

X_LOADS = [2, 2, 4, 8, 16]
X_CHUNKS = [2, 2, 4, 4, 4, 4, 4, 4, 4]
N_PRE = 3
O_CHUNKS = [1] * 4 + [2] * 14
D1 = 3
DT = 7


def a_on_scalar(xc):
    return 1 <= xc <= 3


def e_on_vector(g, half):
    return half == 1 and g >= NT - D1


def starts(sizes):
    return [sum(sizes[:i]) for i in range(len(sizes))]


def tile_trittentioncube_pb_t_kernel(tc, normalized_resid_pre, W_C, b_C, W_K, out):
    nc = tc.nc
    x_v = normalized_resid_pre.rearrange("b t d -> (b t) d").rearrange("(p t) d -> p t d", t=NT)
    out_v = out.rearrange("b t i j -> (b t) (i j)").rearrange("(p t) f -> p t f", t=NT)
    wc_v = W_C.rearrange("n (p t) k -> p n (t k)", t=4)
    wk_v = W_K.rearrange("n i j k -> n (i j) k").rearrange("n (q s) k -> q n (s k)", s=8)
    b_v = b_C.rearrange("n k -> (n k)").rearrange("(p t) -> p t", t=4)
    x_first = starts(X_CHUNKS)
    o_first = starts(O_CHUNKS)
    x_of = [xc for xc, n in enumerate(X_CHUNKS) for a in range(n)]
    o_of = [oc for oc, n in enumerate(O_CHUNKS) for a in range(n)]

    with ExitStack() as ctx:
        keep = ctx.enter_context(tc.tile_pool(name="keep", bufs=1))
        work = ctx.enter_context(tc.tile_pool(name="work", bufs=3))
        xcodes = ctx.enter_context(tc.tile_pool(name="xcodes", bufs=4))
        ccodes = ctx.enter_context(tc.tile_pool(name="ccodes", bufs=6))
        outs = ctx.enter_context(tc.tile_pool(name="outs", bufs=10))
        psum = ctx.enter_context(tc.psum_pool(name="psum", bufs=2))
        ctx.enter_context(tc.manual_schedule())

        x_tiles = []
        x_where = []
        for i, n_tt in enumerate(X_LOADS):
            x_tiles.append(keep.tile([P, n_tt, D], BF16, name="x%d" % i))
            for a in range(n_tt):
                x_where.append((i, a))
        wc_raw = keep.tile([P, 2048], BF16, name="wc_raw")
        b_raw = keep.tile([P, 4], BF16, name="b_raw")
        wk_raw = [keep.tile([P, 8, 256], BF16, name="wk_raw%d" % h) for h in range(2)]

        for h in range(2):
            nc.sync.dma_start(out=wk_raw[h][:], in_=wk_v[:, 8 * h : 8 * h + 8, :])
        nc.sync.dma_start(out=x_tiles[0][:], in_=x_v[:, 0 : X_LOADS[0], :])
        nc.sync.dma_start(out=wc_raw[:].rearrange("p (a b) -> p a b", b=128), in_=wc_v)
        nc.sync.dma_start(out=b_raw[:], in_=b_v)
        t0 = X_LOADS[0]
        for i in range(1, len(X_LOADS)):
            nc.sync.dma_start(out=x_tiles[i][:], in_=x_v[:, t0 : t0 + X_LOADS[i], :])
            t0 += X_LOADS[i]

        ident = keep.tile([P, P], F32, name="ident")
        make_identity(nc, ident[:])

        xg = {}
        xq = {}
        cg = {}
        cq = {}
        pts = {}
        pcs = {}
        pos = {}
        obs = {}

        def t_pe(xc):
            xg[xc] = work.tile([P, 2048], BF16, name="xg", tag="xg", align_bytes=64)
            n = X_CHUNKS[xc]
            for h in range((n + 1) // 2):
                w = min(2, n - 2 * h)
                pt = psum.tile([P, 2, 2 * P], F32, name="pt", tag="pt")
                pts[(xc, h)] = (pt, w)
                for a in range(w):
                    i, loc = x_where[x_first[xc] + 2 * h + a]
                    xw = x_tiles[i][:].bitcast(F32)
                    for u in range(2):
                        nc.tensor.transpose(
                            pt[:, u, a * P : (a + 1) * P], xw[:, loc, u : 2 * P : 2], ident[:]
                        )

        def a_copy(xc, h):
            pt, w = pts[(xc, h)]
            xg_w = xg[xc][:].bitcast(F32).rearrange("p (w u) -> p w u", u=2)
            dst = xg_w[:, h * 2 * P : h * 2 * P + w * P, :]
            src = pt[:, :, 0 : w * P].rearrange("p u w -> p w u")
            if a_on_scalar(xc):
                nc.scalar.copy(out=dst, in_=src)
            else:
                nc.vector.tensor_copy(out=dst, in_=src)

        def qx(xc, h=0):
            if h == 0:
                q = xcodes.tile([P, 512], U32, name="xq", tag="xq", align_bytes=256)
                s = xcodes.tile([P, 512], U8, name="xs", tag="xs", align_bytes=256)
                xq[xc] = (q, s)
            q, s = xq[xc]
            cols = slice(h * 256, (h + 1) * 256)
            nc.vector.quantize_mx(
                out=q[:, cols].bitcast(FP8X4), scales=s[:, cols], in_=xg[xc][:, h * 1024 : (h + 1) * 1024]
            )

        def s1_pe(g):
            q, s = xq[x_of[g]]
            a = g - x_first[x_of[g]]
            blk = slice(a * P, (a + 1) * P)
            pc = psum.tile([P, 4, P], F32, name="pc", tag="pc")
            pcs[g] = pc
            for j in range(4):
                cols = slice(j * P, (j + 1) * P)
                nc.tensor.matmul_mx(
                    out=pc[:, j, :],
                    lhsT=wcq[:, cols].bitcast(FP8X4),
                    lhsT_scale=wcs[:, cols],
                    rhs=q[:, blk].bitcast(FP8X4),
                    rhs_scale=s[:, blk],
                    start=True,
                    stop=True,
                )

        def c_copy(g):
            cg[g] = work.tile([P, P, 4], BF16, name="cg", tag="cg", align_bytes=64)
            nc.vector.tensor_tensor(
                out=cg[g][:],
                in0=pcs[g][:].rearrange("p j r -> p r j"),
                in1=bias[:].unsqueeze(1).to_broadcast([P, P, 4]),
                op=ADD,
            )

        def qc(g):
            q = ccodes.tile([P, P], U32, name="cq", tag="cq", align_bytes=256)
            s = ccodes.tile([P, P], U8, name="cs", tag="cs", align_bytes=256)
            nc.vector.quantize_mx(
                out=q[:].bitcast(FP8X4), scales=s[:], in_=cg[g][:].rearrange("p r j -> p (r j)")
            )
            cq[g] = (q, s)

        def s2_pe(g):
            q, s = cq[g]
            for half in range(2):
                cols = slice(half * 512, (half + 1) * 512)
                po = psum.tile([P, 512], F32, name="po", tag="po", bufs=4)
                pos[(g, half)] = po
                nc.tensor.matmul_mx(
                    out=po[:],
                    lhsT=q[:].bitcast(FP8X4),
                    lhsT_scale=s[:],
                    rhs=wkq[:, cols].bitcast(FP8X4),
                    rhs_scale=wks[:, cols],
                    start=True,
                    stop=True,
                )

        def e_copy(g):
            oc = o_of[g]
            a = g - o_first[oc]
            if a == 0:
                obs[oc] = outs.tile([P, 2, IJ], F32, name="ob", tag="ob")
            for half in range(2):
                cols = slice(half * 512, (half + 1) * 512)
                if e_on_vector(g, half):
                    nc.vector.tensor_copy(out=obs[oc][:, a, cols], in_=pos[(g, half)][:])
                else:
                    nc.scalar.copy(out=obs[oc][:, a, cols], in_=pos[(g, half)][:])
            n = O_CHUNKS[oc]
            if a == n - 1:
                nc.sync.dma_start(out=out_v[:, o_first[oc] : o_first[oc] + n, :], in_=obs[oc][:, 0:n, :])

        wk_s1 = keep.tile([P, 8, 256], F32, name="wk_s1")
        wkg = keep.tile([P, 4 * IJ], BF16, name="wkg", align_bytes=64)
        wkq = keep.tile([P, IJ], U32, name="wkq", align_bytes=256)
        wks = keep.tile([P, IJ], U8, name="wks", align_bytes=256)
        for h in range(2):
            for u in range(2):
                nc.scalar.copy(
                    out=wk_s1[:, :, u * P + h * 64 : u * P + h * 64 + 64].rearrange("p s (n k) -> p s n k", n=8),
                    in_=wk_raw[h][:].bitcast(F32).rearrange("p n (s k u) -> p u s n k", s=8, u=2)[:, u],
                )
        t_pe(0)
        wkg_w = wkg[:].bitcast(F32).rearrange("p (q s u) -> p q s u", s=8, u=2)
        pws = []
        for b in range(4):
            pw = psum.tile([P, 4, P], F32, name="pw", tag="po", bufs=4)
            pws.append(pw)
            for s2 in range(2):
                for u in range(2):
                    nc.tensor.transpose(
                        pw[:, 2 * s2 + u, :], wk_s1[:, 2 * b + s2, u * P : (u + 1) * P], ident[:]
                    )
        for xc in range(1, N_PRE):
            t_pe(xc)
        a_copy(0, 0)
        qx(0)
        for b in range(4):
            nc.scalar.copy(
                out=wkg_w[:, :, 2 * b : 2 * b + 2, :], in_=pws[b][:].rearrange("p (s u) q -> p q s u", u=2)
            )
        for xc in range(1, N_PRE):
            for h in range((X_CHUNKS[xc] + 1) // 2):
                a_copy(xc, h)

        bias = keep.tile([P, 4], F32, name="bias")
        wcg = keep.tile([P, 2048], BF16, name="wcg", align_bytes=64)
        wcq = keep.tile([P, 512], U32, name="wcq", align_bytes=256)
        wcs = keep.tile([P, 512], U8, name="wcs", align_bytes=256)
        raw_v = wc_raw[:].rearrange("p (n t k j) -> p j n k t", n=16, t=4, j=4)
        wcg_v = wcg[:].rearrange("p (j n k t) -> p j n k t", j=4, n=16, t=4)
        for j in range(4):
            nc.vector.tensor_copy(out=wcg_v[:, j], in_=raw_v[:, j])
        nc.vector.quantize_mx(out=wcq[:].bitcast(FP8X4), scales=wcs[:], in_=wcg[:])
        nc.vector.tensor_copy(out=bias[:], in_=b_raw[:])
        nc.vector.quantize_mx(out=wkq[:].bitcast(FP8X4), scales=wks[:], in_=wkg[:])

        t_tick = [-1 if xc < N_PRE else 1 + 14 * (xc - N_PRE) // 3 for xc in range(len(X_CHUNKS))]
        for g1 in range(NT + D1):
            g = g1 - D1
            if g >= 0:
                s2_pe(g)
            if g1 < NT:
                s1_pe(g1)
            for xc in range(N_PRE, len(X_CHUNKS)):
                if t_tick[xc] == g1:
                    t_pe(xc)
            if g1 < NT:
                c_copy(g1)
            if g1 == 0:
                qx(1)
            if g1 == 2:
                qx(2)
                qx(2, 1)
            for xc in range(N_PRE, len(X_CHUNKS)):
                if t_tick[xc] == g1:
                    a_copy(xc, 0)
                if t_tick[xc] + 1 == g1:
                    a_copy(xc, 1)
                for h in range(2):
                    if t_tick[xc] + 2 + h == g1:
                        qx(xc, h)
            if g1 < NT:
                qc(g1)
            if g >= 0:
                e_copy(g)
